import numpy as np
import ml_dtypes


def mxq(x, axis, fmt="e4m3"):
    dtype, down = {"e4m3": (ml_dtypes.float8_e4m3fn, 7), "e5m2": (ml_dtypes.float8_e5m2, 14)}[fmt]
    v = np.moveaxis(np.asarray(x, np.float32).astype(ml_dtypes.bfloat16).astype(np.float64), axis, -1)
    blocks = v.reshape(v.shape[:-1] + (-1, 32))
    amax = np.abs(blocks).max(-1, keepdims=True)
    byte = np.maximum(np.where(amax > 0, np.frexp(amax)[1] - 1 + 127, 0) - down, 1)
    scale = np.exp2(byte - 127.0)
    codes = (blocks / scale).astype(np.float32).astype(dtype).astype(np.float64)
    return np.moveaxis((codes * scale).reshape(v.shape), -1, axis)


WIDE = False


def mx_kscale(k):
    if not WIDE:
        return np.ones(k)
    levels = np.array([18, -18])
    if k % 512:
        return np.exp2(np.random.permutation(np.resize(levels, k // 32))).repeat(32)
    a = np.empty((k // 512, 16))
    for p in range(k // 512):
        a[p, :8] = np.random.permutation(np.resize(levels, 8))
        for g in range(8):
            far = levels[np.abs(levels - a[p, g]) >= 10]
            a[p, g + 8] = far[np.random.randint(len(far))]
    return np.exp2(a.ravel()).repeat(32)


BF16 = ml_dtypes.bfloat16


def bf(x):
    return np.asarray(x, np.float32).astype(BF16)


def f64(x):
    return np.asarray(x).astype(np.float64)


B, S, E, H, KV, D = 1, 512, 1536, 12, 4, 128
D2 = D // 2
T = B * S
JQ, JK = H * D, KV * D
THETA = 10000.0


def rope_back(g, cos, sin):
    g1, g2 = g[..., :D2], g[..., D2:]
    c = cos[None, :, None, :]
    s = sin[None, :, None, :]
    return np.concatenate([g1 * c + g2 * s, g2 * c - g1 * s], axis=-1)


def pair_scale(j):
    u = mx_kscale(j)[:j // 2].reshape(j // D, 1, D2)
    return np.concatenate([u, u], axis=1).reshape(j)


def setup_inputs():
    s = mx_kscale(T)
    uq = pair_scale(JQ)
    uk = pair_scale(JK)
    uv = mx_kscale(JK)
    ang = np.outer(np.arange(S), 1.0 / THETA ** (np.arange(0, D, 2) / D))
    x = bf(np.random.standard_normal((B, S, E)) * s.reshape(B, S, 1))
    wq = bf(np.random.standard_normal((E, JQ)) * 1.5 / np.sqrt(E) / uq)
    wk = bf(np.random.standard_normal((E, JK)) * 1.5 / np.sqrt(E) / uk)
    wv = bf(np.random.standard_normal((E, JK)) * 1.0 / np.sqrt(E) / uv)
    st = s.reshape(B, S, 1, 1)
    g0 = bf(np.random.standard_normal((B, S, H, D)) * np.exp2(np.random.randint(-6, 1, (B, S, 1, 1))) / st * uq.reshape(H, D))
    g1 = bf(np.random.standard_normal((B, S, KV, D)) * np.exp2(np.random.randint(-6, 1, (B, S, 1, 1))) / st * uk.reshape(KV, D))
    g2 = bf(np.random.standard_normal((B, S, KV, D)) * np.exp2(np.random.randint(-6, 1, (B, S, 1, 1))) / st * uv.reshape(KV, D))
    return {"x": x, "wq": wq, "wk": wk, "wv": wv,
            "freqs_cos": bf(np.cos(ang)), "freqs_sin": bf(np.sin(ang)),
            "grad_0": g0, "grad_1": g1, "grad_2": g2}


def reference(x, wq, wk, wv, freqs_cos, freqs_sin, grad_0, grad_1, grad_2):
    cos, sin = f64(freqs_cos), f64(freqs_sin)
    dq = rope_back(f64(grad_0), cos, sin).reshape(T, JQ)
    dk = rope_back(f64(grad_1), cos, sin).reshape(T, JK)
    dv = f64(grad_2).reshape(T, JK)
    dz = np.concatenate([dq, dk, dv], axis=1)
    w = np.concatenate([f64(wq), f64(wk), f64(wv)], axis=1)
    dx = mxq(dz, 1, "e5m2") @ mxq(w, 1, "e4m3").T
    xt = mxq(f64(x).reshape(T, E), 0, "e4m3")
    dw = xt.T @ mxq(dz, 0, "e5m2")
    return dx.reshape(B, S, E), dw[:, :JQ], dw[:, JQ:JQ + JK], dw[:, JQ + JK:]

@@ -1,0 +1,333 @@
+from contextlib import ExitStack
+
+import concourse.mybir as mybir
+from concourse.masks import make_identity
+
+T, E, D2 = 512, 1536, 64
+JQ, JK = 1536, 512
+FLOPS = 2 * 2 * T * E * (JQ + 2 * JK)
+
+F32 = mybir.dt.float32
+BF16 = mybir.dt.bfloat16
+U32 = mybir.dt.uint32
+U8 = mybir.dt.uint8
+E4M3 = mybir.dt.float8_e4m3fn_x4
+E5M2 = mybir.dt.float8_e5m2_x4
+ALU = mybir.AluOpType
+
+P = 128
+PACK = 4
+N = 512
+CHUNKS = E // N
+
+
+def tile_llamaattentionfused_pa_v_kernel(
+    tc, x, wq, wk, wv, freqs_cos, freqs_sin, grad_0, grad_1, grad_2, out_0, out_1, out_2, out_3
+):
+    nc = tc.nc
+    with ExitStack() as ctx:
+        sb = ctx.enter_context(tc.tile_pool(name="sb", bufs=1))
+        psum = ctx.enter_context(tc.psum_pool(name="psum", bufs=8))
+        ctx.enter_context(tc.manual_schedule())
+
+        ident = sb.tile([P, P], F32, name="ident")
+        make_identity(nc, ident[:])
+
+        def copy(engine, out, in_):
+            if engine == "vector":
+                nc.vector.tensor_copy(out=out, in_=in_)
+            else:
+                nc.scalar.copy(out=out, in_=in_)
+
+        def load(name, src, tag, bufs):
+            t = sb.tile([P, src.shape[1]], BF16, name=name, tag=tag, bufs=bufs, align_bytes=64)
+            nc.sync.dma_start(out=t[:], in_=src)
+            return t[:].rearrange("p (j c) -> p j c", j=PACK)
+
+        def load_wide(name, src):
+            return load(name, src, "wide", 4)
+
+        def load_narrow(name, src):
+            return load(name, src, "narrow", 6)
+
+        def weight_rows(w, n):
+            return w[N * n : N * (n + 1), :].rearrange("(p r) c -> p (r c)", r=PACK)
+
+        def grouped_tile(name, width=PACK * N):
+            t = sb.tile([P, width], BF16, name=name, tag="grouped", bufs=5, align_bytes=64)
+            return t
+
+        def quantize(name, grouped, fmt):
+            width = grouped.shape[1] // PACK
+            codes = sb.tile([P, width], U32, name=name + "_codes", align_bytes=64)
+            scales = sb.tile([P, width], U8, name=name + "_scales", align_bytes=64)
+            nc.vector.quantize_mx(out=codes[:].bitcast(fmt), scales=scales[:], in_=grouped[:])
+            return codes, scales, fmt
+
+        def matmul(out, stationary, col, moving, start, stop):
+            cols = slice(col, col + P)
+            nc.tensor.matmul_mx(
+                out=out,
+                lhsT=stationary[0][:, cols].bitcast(stationary[2]),
+                lhsT_scale=stationary[1][:, cols],
+                rhs=moving[0][:].bitcast(moving[2]),
+                rhs_scale=moving[1][:],
+                start=start,
+                stop=stop,
+            )
+
+        def rope_products(name, g, j0):
+            slots, width = g.shape[1], g.shape[2]
+            prods = []
+            for kind, table in (("cos", cos), ("sin", sin)):
+                prod = sb.tile([P, slots * width], F32, name=name + kind, tag="prod_" + kind, bufs=1)
+                nc.vector.tensor_tensor(
+                    out=prod[:].rearrange("p (j h i) -> p j h i", j=slots, i=D2),
+                    in0=g.rearrange("p j (h i) -> p j h i", i=D2),
+                    in1=table[:, j0 : j0 + slots, :].unsqueeze(2).to_broadcast([P, slots, width // D2, D2]),
+                    op=ALU.mult,
+                )
+                prods.append(prod[:].rearrange("p (j h two i) -> p j h two i", j=slots, two=2, i=D2))
+            return prods
+
+        def rope_sums(prods, dz):
+            gc, gs = prods
+            halves = dz.rearrange("p j (h two i) -> p j h two i", two=2, i=D2)
+            nc.vector.tensor_tensor(out=halves[:, :, :, 0, :], in0=gc[:, :, :, 0, :], in1=gs[:, :, :, 1, :], op=ALU.add)
+            nc.vector.tensor_tensor(out=halves[:, :, :, 1, :], in0=gc[:, :, :, 1, :], in1=gs[:, :, :, 0, :], op=ALU.subtract)
+
+        def group_tokens(engine, name, rows):
+            grouped = grouped_tile(name)
+            copy(
+                engine,
+                grouped[:].rearrange("p (c i j) -> p c j i", i=4, j=PACK),
+                rows.rearrange("p j (c i) -> p c j i", i=4),
+            )
+            return grouped
+
+        def group_x(engine, n):
+            grouped = grouped_tile("x_grouped%d" % n)
+            copy(
+                engine,
+                grouped[:].rearrange("p (r m j) -> p m j r", r=PACK, j=PACK),
+                x_rows[:, :, N * n : N * (n + 1)].rearrange("p j (m r) -> p m j r", r=PACK),
+            )
+            return grouped
+
+        def transpose_pair(engine, name, sources, grouped, half):
+            bank = psum.tile([P, 2, 2, P], F32, name=name, tag="bank")
+            for s, src in enumerate(sources):
+                words = src.bitcast(F32)
+                for u in range(2):
+                    nc.tensor.transpose(bank[:, s, u, :], words[:, u::2], ident[:])
+            dst = grouped[:].bitcast(F32)[:, N * half : N * (half + 1)]
+            return lambda: copy(engine, dst.rearrange("p (s r u) -> p s r u", s=2, u=2), bank[:].rearrange("p s u r -> p s r u"))
+
+        def transpose_rows(engines, name, rows):
+            grouped = grouped_tile(name)
+            outs = [
+                transpose_pair(engines[h], name + "_bank%d" % h, [rows[:, 2 * h, :], rows[:, 2 * h + 1, :]], grouped, h)
+                for h in range(2)
+            ]
+            for o in outs:
+                o()
+            return grouped
+
+        def stage_tile(name, width):
+            t = sb.tile([P, width], F32, name=name, tag="stage", bufs=5)
+            return t
+
+        def dw_bank(engine, name, n, r, dz, dst):
+            bank = psum.tile([P, N], F32, name=name, tag="bank")
+            matmul(bank[:], x_mx[n], P * r, dz, True, True)
+            copy(engine, dst, bank[:])
+
+        def dw_chunk(engines, name, n, dz, out_cols):
+            stage = stage_tile(name, PACK * N)
+            for r in range(PACK):
+                dw_bank(engines[r], name + "_bank%d" % r, n, r, dz, stage[:, N * r : N * (r + 1)])
+            return lambda: nc.sync.dma_start(
+                out=out_cols[N * n : N * (n + 1), :].rearrange("(m r) c -> m r c", r=PACK),
+                in_=stage[:].rearrange("p (r c) -> p r c", r=PACK),
+            )
+
+        def dw_pair(engines, n, half):
+            name = "dwq_%d_%d" % (n, half)
+            stage = stage_tile(name, PACK * N)
+            for s in range(2):
+                for c in range(2):
+                    i = 2 * s + c
+                    dw_bank(engines[i], name + "_bank%d" % i, n, 2 * half + s, dz_tok["q%d" % (c + 1)], stage[:, N * i : N * (i + 1)])
+            rows = out_1[N * n : N * (n + 1), N:].rearrange("(m r) c -> m r c", r=PACK)
+            nc.sync.dma_start(out=rows[:, 2 * half : 2 * half + 2, :], in_=stage[:].rearrange("p (r c) -> p r c", r=2))
+
+        def dwq_rows(engines, n, r):
+            name = "dwq_%d_%d" % (n, r)
+            stage = stage_tile(name, JQ)
+            for c in range(3):
+                dw_bank(engines[c], name + "_bank%d" % c, n, r, dz_tok["q%d" % c], stage[:, N * c : N * (c + 1)])
+            rows = out_1[N * n : N * (n + 1), :].rearrange("(m r) c -> m r c", r=PACK)
+            nc.sync.dma_start(out=rows[:, r, :], in_=stage[:])
+
+        def dx_banks(engines, j, ns):
+            stage = stage_tile("dx%d_%d" % (j, ns[0]), N * len(ns))
+            for s, n in enumerate(ns):
+                bank = psum.tile([P, N], F32, name="dx%d_bank%d" % (j, n), tag="bank")
+                terms = [(dz_feat["v"], P * j, w_mx["v", n])]
+                terms += [(dz_slot[j], P * i, w_mx[c, n]) for i, c in enumerate(("q0", "q1", "q2", "k"))]
+                for i, (stationary, col, moving) in enumerate(terms):
+                    matmul(bank[:], stationary, col, moving, i == 0, i == len(terms) - 1)
+                copy(
+                    engines[s],
+                    stage[:, N * s : N * (s + 1)].rearrange("p (m r) -> p m r", r=PACK),
+                    bank[:].rearrange("p (r m) -> p m r", r=PACK),
+                )
+            rows = out_0.rearrange("b (p j) e -> p (b j) e", j=PACK)
+            nc.sync.dma_start(out=rows[:, j, N * ns[0] : N * (ns[-1] + 1)], in_=stage[:])
+
+        def token_rows(g):
+            return g.rearrange("b (p j) h d -> p (b j h d)", j=PACK)
+
+        S, V = "scalar", "vector"
+        x_mx, dz_tok, dz_feat, dz_slot, w_mx, w_rows, w_grouped = {}, {}, {}, {}, {}, {}, {}
+
+        def load_weights(n):
+            w_rows["v", n] = load_narrow("wv%d" % n, weight_rows(wv, n))
+            w_rows["k", n] = load_narrow("wk%d" % n, weight_rows(wk, n))
+            load_wq(n)
+
+        def load_wq(n):
+            rows = load_wide("wq%d" % n, weight_rows(wq, n))
+            for i in range(3):
+                w_rows["q%d" % i, n] = rows[:, :, N * i : N * (i + 1)]
+
+        def turn_w(c, n, engines=(S, S)):
+            w_grouped[c, n] = transpose_rows(engines, "w%s%d_grouped" % (c, n), w_rows[c, n])
+
+        def quantize_w(c, n):
+            w_mx[c, n] = quantize("w%s%d" % (c, n), w_grouped[c, n], E4M3)
+
+
+        cos = load("cos", freqs_cos.rearrange("(p j) i -> p (j i)", j=PACK), "cos", 1)
+        sin = load("sin", freqs_sin.rearrange("(p j) i -> p (j i)", j=PACK), "sin", 1)
+        gk = load_narrow("gk", token_rows(grad_1))
+        gv = load_narrow("gv", token_rows(grad_2))
+        x_rows = load_wide("x", x.rearrange("b (p j) e -> p (b j e)", j=PACK))
+        w_rows["v", 0] = load_narrow("wv0", weight_rows(wv, 0))
+        w_rows["k", 0] = load_narrow("wk0", weight_rows(wk, 0))
+        gq = load_wide("gq", token_rows(grad_0))
+        load_wq(0)
+        load_weights(1)
+
+        SSSS = (S, S, S, S)
+        SV = (S, V, S, V)
+        VS = (V, S, V, S)
+        dzk_tile = sb.tile([P, PACK * N], BF16, name="dzk", align_bytes=64)
+        dzk = dzk_tile[:].rearrange("p (j c) -> p j c", j=PACK)
+        dzq_tile = sb.tile([P, PACK * JQ], BF16, name="dzq", align_bytes=64)
+        dzq = dzq_tile[:].rearrange("p (j c) -> p j c", j=PACK)
+
+        def slot_turn(j, engines=(S, S)):
+            grouped = grouped_tile("slot%d_grouped" % j)
+            a = transpose_pair(engines[0], "slot%d_a" % j, [dzq[:, j, :N], dzq[:, j, N : 2 * N]], grouped, 0)
+            b = transpose_pair(engines[1], "slot%d_b" % j, [dzq[:, j, 2 * N :], dzk[:, j, :]], grouped, 1)
+            a()
+            b()
+            return grouped
+
+        pr = rope_products("k", gk, 0)
+        v_tok = group_tokens(S, "v_tok", gv)
+        v_feat = transpose_rows((S, S), "v_feat", gv)
+        x0 = group_x(S, 0)
+        dz_tok["v"] = quantize("v_tok", v_tok, E5M2)
+        rope_sums(pr, dzk)
+        dz_feat["v"] = quantize("v_feat", v_feat, E5M2)
+        k_tok = group_tokens(V, "k_tok", dzk)
+        x1 = group_x(S, 1)
+        x_mx[0] = quantize("x0", x0, E4M3)
+        x2 = group_x(V, 2)
+        dz_tok["k"] = quantize("k_tok", k_tok, E5M2)
+        turn_w("v", 0)
+        turn_w("k", 0)
+        load_weights(2)
+        x_mx[1] = quantize("x1", x1, E4M3)
+        x_mx[2] = quantize("x2", x2, E4M3)
+        dw_chunk(SSSS, "dwv0", 0, dz_tok["v"], out_3)()
+
+        pr = rope_products("s0", gq[:, 0:1, :], 0)
+        turn_w("q0", 0)
+        turn_w("q1", 0)
+        turn_w("q2", 0)
+        quantize_w("v", 0)
+        quantize_w("k", 0)
+        rope_sums(pr, dzq[:, 0:1, :])
+        dw_chunk(SSSS, "dwv1", 1, dz_tok["v"], out_3)()
+        g0 = slot_turn(0)
+        turn_w("v", 1)
+        quantize_w("q0", 0)
+        quantize_w("q1", 0)
+        quantize_w("q2", 0)
+        turn_w("k", 1)
+        turn_w("q0", 1)
+
+        pr = rope_products("s1", gq[:, 1:2, :], 1)
+        dz_slot[0] = quantize("slot0", g0, E5M2)
+        quantize_w("v", 1)
+        rope_sums(pr, dzq[:, 1:2, :])
+        turn_w("q1", 1)
+        turn_w("q2", 1)
+        dx_banks(SSSS, 0, (0,))
+        dw_chunk(SSSS, "dwv2", 2, dz_tok["v"], out_3)()
+        quantize_w("k", 1)
+        quantize_w("q0", 1)
+        quantize_w("q1", 1)
+        g1 = slot_turn(1)
+
+        pr = rope_products("s2", gq[:, 2:3, :], 2)
+        quantize_w("q2", 1)
+        dz_slot[1] = quantize("slot1", g1, E5M2)
+        dw_chunk(SSSS, "dwk0", 0, dz_tok["k"], out_2)()
+        rope_sums(pr, dzq[:, 2:3, :])
+        dx_banks(SSSS, 0, (1,))
+        dw_chunk(SSSS, "dwk1", 1, dz_tok["k"], out_2)()
+        g2 = slot_turn(2)
+        dx_banks(SSSS, 1, (0, 1))
+
+        pr = rope_products("s3a", gq[:, 3:4, :N], 3)
+        rope_sums(pr, dzq[:, 3:4, :N])
+        pr = rope_products("s3b", gq[:, 3:4, N:], 3)
+        q0_tok = group_tokens(V, "q0_tok", dzq[:, :, :N])
+        dz_slot[2] = quantize("slot2", g2, E5M2)
+        dz_tok["q0"] = quantize("q0_tok", q0_tok, E5M2)
+        dw_chunk(SSSS, "dwk2", 2, dz_tok["k"], out_2)()
+        rope_sums(pr, dzq[:, 3:4, N:])
+        dx_banks(SSSS, 2, (0, 1))
+        dw_chunk(SSSS, "dwq00", 0, dz_tok["q0"], out_1[:, :N])()
+        turn_w("v", 2, (V, V))
+        q1_tok = group_tokens(V, "q1_tok", dzq[:, :, N : 2 * N])
+        quantize_w("v", 2)
+        turn_w("k", 2, (V, V))
+        dz_tok["q1"] = quantize("q1_tok", q1_tok, E5M2)
+        dw_chunk(SSSS, "dwq01", 1, dz_tok["q0"], out_1[:, :N])()
+        q2_tok = group_tokens(V, "q2_tok", dzq[:, :, 2 * N :])
+        quantize_w("k", 2)
+        turn_w("q0", 2, (V, V))
+        dz_tok["q2"] = quantize("q2_tok", q2_tok, E5M2)
+        dw_chunk(SSSS, "dwq02", 2, dz_tok["q0"], out_1[:, :N])()
+        turn_w("q1", 2, (V, V))
+        quantize_w("q0", 2)
+        dw_pair(SSSS, 0, 0)
+        turn_w("q2", 2, (V, V))
+        quantize_w("q1", 2)
+        g3 = slot_turn(3, (V, V))
+        quantize_w("q2", 2)
+        dw_pair(SSSS, 0, 1)
+        dz_slot[3] = quantize("slot3", g3, E5M2)
+        dx_banks(VS, 0, (2,))
+        dw_pair(SV, 1, 0)
+        dx_banks(VS, 1, (2,))
+        dw_pair(SV, 1, 1)
+        dx_banks(VS, 2, (2,))
+        dw_pair(SV, 2, 0)
+        dx_banks(VS, 3, (0, 1, 2))
+        dw_pair(SV, 2, 1)

@@ -27,7 +27,8 @@ def tile_llamaattentionfused_pa_v_kernel(
     nc = tc.nc
     with ExitStack() as ctx:
         sb = ctx.enter_context(tc.tile_pool(name="sb", bufs=1))
-        psum = ctx.enter_context(tc.psum_pool(name="psum", bufs=8))
+        psum = ctx.enter_context(tc.psum_pool(name="psum", bufs=7))
+        psum_keep = ctx.enter_context(tc.psum_pool(name="psum_keep", bufs=1))
         ctx.enter_context(tc.manual_schedule())
 
         ident = sb.tile([P, P], F32, name="ident")
@@ -48,13 +49,17 @@ def tile_llamaattentionfused_pa_v_kernel(
             return load(name, src, "wide", 4)
 
         def load_narrow(name, src):
-            return load(name, src, "narrow", 6)
+            return load(name, src, "narrow", 4)
 
         def weight_rows(w, n):
             return w[N * n : N * (n + 1), :].rearrange("(p r) c -> p (r c)", r=PACK)
 
         def grouped_tile(name, width=PACK * N):
             t = sb.tile([P, width], BF16, name=name, tag="grouped", bufs=5, align_bytes=64)
+            return t
+
+        def spare_tile(name):
+            t = sb.tile([P, PACK * N], BF16, name=name, tag="narrow", bufs=4, align_bytes=64)
             return t
 
         def quantize(name, grouped, fmt):
@@ -76,28 +81,44 @@ def tile_llamaattentionfused_pa_v_kernel(
                 stop=stop,
             )
 
-        def rope_products(name, g, j0):
+        def table_view(tables, kind, j0, slots, reps):
+            rows = tables.rearrange("p (k j i) -> p k j i", k=3, i=D2)[:, kind, j0 : j0 + slots, :]
+            return rows.unsqueeze(2).to_broadcast([P, slots, reps, D2])
+
+        def cos_product(name, tables, g, j0):
             slots, width = g.shape[1], g.shape[2]
-            prods = []
-            for kind, table in (("cos", cos), ("sin", sin)):
-                prod = sb.tile([P, slots * width], F32, name=name + kind, tag="prod_" + kind, bufs=1)
+            prod = sb.tile([P, slots * width], F32, name=name + "_cos", tag="prod_cos", bufs=2)
+            nc.vector.tensor_tensor(
+                out=prod[:].rearrange("p (j h i) -> p j h i", j=slots, i=D2),
+                in0=g.rearrange("p j (h i) -> p j h i", i=D2),
+                in1=table_view(tables, 0, j0, slots, width // D2),
+                op=ALU.mult,
+            )
+            return prod
+
+        def sin_product(name, tables, g, j0):
+            slots, width = g.shape[1], g.shape[2]
+            prod = sb.tile([P, slots * width], F32, name=name + "_sin", tag="prod_sin", bufs=2)
+            for half in range(2):
                 nc.vector.tensor_tensor(
-                    out=prod[:].rearrange("p (j h i) -> p j h i", j=slots, i=D2),
-                    in0=g.rearrange("p j (h i) -> p j h i", i=D2),
-                    in1=table[:, j0 : j0 + slots, :].unsqueeze(2).to_broadcast([P, slots, width // D2, D2]),
+                    out=prod[:].rearrange("p (j h two i) -> p j h two i", j=slots, two=2, i=D2)[:, :, :, half, :],
+                    in0=g.rearrange("p j (h two i) -> p j h two i", two=2, i=D2)[:, :, :, 1 - half, :],
+                    in1=table_view(tables, 1 + half, j0, slots, width // (2 * D2)),
                     op=ALU.mult,
                 )
-                prods.append(prod[:].rearrange("p (j h two i) -> p j h two i", j=slots, two=2, i=D2))
-            return prods
+            return prod
 
-        def rope_sums(prods, dz):
-            gc, gs = prods
-            halves = dz.rearrange("p j (h two i) -> p j h two i", two=2, i=D2)
-            nc.vector.tensor_tensor(out=halves[:, :, :, 0, :], in0=gc[:, :, :, 0, :], in1=gs[:, :, :, 1, :], op=ALU.add)
-            nc.vector.tensor_tensor(out=halves[:, :, :, 1, :], in0=gc[:, :, :, 1, :], in1=gs[:, :, :, 0, :], op=ALU.subtract)
+        def rope_sum(engine, a, b, dz):
+            slots = dz.shape[1]
+            engine.tensor_tensor(
+                out=dz,
+                in0=a[:].rearrange("p (j c) -> p j c", j=slots),
+                in1=b[:].rearrange("p (j c) -> p j c", j=slots),
+                op=ALU.add,
+            )
 
-        def group_tokens(engine, name, rows):
-            grouped = grouped_tile(name)
+        def group_tokens(engine, name, rows, late=False):
+            grouped = spare_tile(name) if late else grouped_tile(name)
             copy(
                 engine,
                 grouped[:].rearrange("p (c i j) -> p c j i", i=4, j=PACK),
@@ -174,7 +195,7 @@ def tile_llamaattentionfused_pa_v_kernel(
             for s, n in enumerate(ns):
                 bank = psum.tile([P, N], F32, name="dx%d_bank%d" % (j, n), tag="bank")
                 terms = [(dz_feat["v"], P * j, w_mx["v", n])]
-                terms += [(dz_slot[j], P * i, w_mx[c, n]) for i, c in enumerate(("q0", "q1", "q2", "k"))]
+                terms += [(dz_slot[j], P * i, w_mx[c, n]) for i, c in enumerate(("k", "q0", "q1", "q2"))]
                 for i, (stationary, col, moving) in enumerate(terms):
                     matmul(bank[:], stationary, col, moving, i == 0, i == len(terms) - 1)
                 copy(
@@ -208,16 +229,16 @@ def tile_llamaattentionfused_pa_v_kernel(
             w_mx[c, n] = quantize("w%s%d" % (c, n), w_grouped[c, n], E4M3)
 
 
-        cos = load("cos", freqs_cos.rearrange("(p j) i -> p (j i)", j=PACK), "cos", 1)
-        sin = load("sin", freqs_sin.rearrange("(p j) i -> p (j i)", j=PACK), "sin", 1)
+        TAB = PACK * D2
+        tables = sb.tile([P, 3 * TAB], BF16, name="tables", align_bytes=64)
+        nc.sync.dma_start(out=tables[:, :TAB], in_=freqs_cos.rearrange("(p j) i -> p (j i)", j=PACK))
+        nc.sync.dma_start(out=tables[:, TAB : 2 * TAB], in_=freqs_sin.rearrange("(p j) i -> p (j i)", j=PACK))
         gk = load_narrow("gk", token_rows(grad_1))
         gv = load_narrow("gv", token_rows(grad_2))
-        x_rows = load_wide("x", x.rearrange("b (p j) e -> p (b j e)", j=PACK))
-        w_rows["v", 0] = load_narrow("wv0", weight_rows(wv, 0))
         w_rows["k", 0] = load_narrow("wk0", weight_rows(wk, 0))
-        gq = load_wide("gq", token_rows(grad_0))
+        w_rows["v", 0] = load_narrow("wv0", weight_rows(wv, 0))
+        x_rows = load_wide("x", x.rearrange("b (p j) e -> p (b j e)", j=PACK))
         load_wq(0)
-        load_weights(1)
 
         SSSS = (S, S, S, S)
         SV = (S, V, S, V)
@@ -229,105 +250,130 @@ def tile_llamaattentionfused_pa_v_kernel(
 
         def slot_turn(j, engines=(S, S)):
             grouped = grouped_tile("slot%d_grouped" % j)
-            a = transpose_pair(engines[0], "slot%d_a" % j, [dzq[:, j, :N], dzq[:, j, N : 2 * N]], grouped, 0)
-            b = transpose_pair(engines[1], "slot%d_b" % j, [dzq[:, j, 2 * N :], dzk[:, j, :]], grouped, 1)
+            a = transpose_pair(engines[0], "slot%d_a" % j, [dzk[:, j, :], dzq[:, j, :N]], grouped, 0)
+            b = transpose_pair(engines[1], "slot%d_b" % j, [dzq[:, j, N : 2 * N], dzq[:, j, 2 * N :]], grouped, 1)
             a()
             b()
             return grouped
 
-        pr = rope_products("k", gk, 0)
+        nc.vector.tensor_scalar(out=tables[:, 2 * TAB :], in0=tables[:, TAB : 2 * TAB], scalar1=-1.0, scalar2=None, op0=ALU.mult)
+        turned_bank = psum.tile([P, 3, P], F32, name="turned_bank", tag="bank")
+        turned = sb.tile([P, 3, P], F32, name="turned")
+        table_bank = psum_keep.tile([P, 3 * P], F32, name="table_bank")
+        for kind in range(3):
+            nc.tensor.transpose(turned_bank[:, kind, :], tables[:].bitcast(F32)[:, P * kind : P * (kind + 1)], ident[:])
+        nc.scalar.copy(out=turned[:], in_=turned_bank[:])
+        for kind in range(3):
+            nc.tensor.transpose(table_bank[:, P * kind : P * (kind + 1)], turned[:, kind, :], ident[:])
+        psum_tables = table_bank[:].bitcast(BF16)
+
+        G = nc.gpsimd
+        a = cos_product("k0", tables[:], gk[:, 0:2, :], 0)
+        b = sin_product("k0", tables[:], gk[:, 0:2, :], 0)
+        a1 = cos_product("k1", tables[:], gk[:, 2:4, :], 2)
+        rope_sum(nc.vector, a, b, dzk[:, 0:2, :])
         v_tok = group_tokens(S, "v_tok", gv)
         v_feat = transpose_rows((S, S), "v_feat", gv)
-        x0 = group_x(S, 0)
         dz_tok["v"] = quantize("v_tok", v_tok, E5M2)
-        rope_sums(pr, dzk)
-        dz_feat["v"] = quantize("v_feat", v_feat, E5M2)
-        k_tok = group_tokens(V, "k_tok", dzk)
-        x1 = group_x(S, 1)
-        x_mx[0] = quantize("x0", x0, E4M3)
-        x2 = group_x(V, 2)
-        dz_tok["k"] = quantize("k_tok", k_tok, E5M2)
-        turn_w("v", 0)
+        b1 = sin_product("k1", tables[:], gk[:, 2:4, :], 2)
         turn_w("k", 0)
+        turn_w("v", 0)
+        dz_feat["v"] = quantize("v_feat", v_feat, E5M2)
+        rope_sum(nc.vector, a1, b1, dzk[:, 2:4, :])
+        quantize_w("k", 0)
+        w_rows["v", 1] = load_narrow("wv1", weight_rows(wv, 1))
+        w_rows["k", 1] = load_narrow("wk1", weight_rows(wk, 1))
+        gq = load_wide("gq", token_rows(grad_0))
+        load_wq(1)
+        x0 = group_x(S, 0)
+        k_tok = group_tokens(V, "k_tok", dzk)
+        quantize_w("v", 0)
+        dz_tok["k"] = quantize("k_tok", k_tok, E5M2)
+        x_mx[0] = quantize("x0", x0, E4M3)
+        x1 = group_x(S, 1)
+        x2 = group_x(V, 2)
         load_weights(2)
         x_mx[1] = quantize("x1", x1, E4M3)
-        x_mx[2] = quantize("x2", x2, E4M3)
-        dw_chunk(SSSS, "dwv0", 0, dz_tok["v"], out_3)()
-
-        pr = rope_products("s0", gq[:, 0:1, :], 0)
         turn_w("q0", 0)
         turn_w("q1", 0)
         turn_w("q2", 0)
-        quantize_w("v", 0)
-        quantize_w("k", 0)
-        rope_sums(pr, dzq[:, 0:1, :])
-        dw_chunk(SSSS, "dwv1", 1, dz_tok["v"], out_3)()
-        g0 = slot_turn(0)
-        turn_w("v", 1)
+        x_mx[2] = quantize("x2", x2, E4M3)
         quantize_w("q0", 0)
         quantize_w("q1", 0)
-        quantize_w("q2", 0)
+        dw_chunk(SSSS, "dwk0", 0, dz_tok["k"], out_2)()
+        turn_w("v", 1)
         turn_w("k", 1)
-        turn_w("q0", 1)
+        dw_chunk(SSSS, "dwv0", 0, dz_tok["v"], out_3)()
 
-        pr = rope_products("s1", gq[:, 1:2, :], 1)
+        a = cos_product("s0", psum_tables, gq[:, 0:1, :], 0)
+        quantize_w("q2", 0)
+        b = sin_product("s0", psum_tables, gq[:, 0:1, :], 0)
+        rope_sum(G, a, b, dzq[:, 0:1, :])
+        a = cos_product("q0", psum_tables, gq[:, 1:4, :N], 1)
+        b = sin_product("q0", psum_tables, gq[:, 1:4, :N], 1)
+        rope_sum(G, a, b, dzq[:, 1:4, :N])
+        a = cos_product("s1", psum_tables, gq[:, 1:2, N:], 1)
+        dw_chunk(SSSS, "dwk1", 1, dz_tok["k"], out_2)()
+        turn_w("q0", 1, (V, V))
+        g0 = slot_turn(0)
+        turn_w("q1", 1, (V, V))
+        dw_chunk(SSSS, "dwv1", 1, dz_tok["v"], out_3)()
         dz_slot[0] = quantize("slot0", g0, E5M2)
         quantize_w("v", 1)
-        rope_sums(pr, dzq[:, 1:2, :])
-        turn_w("q1", 1)
         turn_w("q2", 1)
-        dx_banks(SSSS, 0, (0,))
-        dw_chunk(SSSS, "dwv2", 2, dz_tok["v"], out_3)()
         quantize_w("k", 1)
+        q0_tok = group_tokens(V, "q0_tok", dzq[:, :, :N])
         quantize_w("q0", 1)
         quantize_w("q1", 1)
-        g1 = slot_turn(1)
-
-        pr = rope_products("s2", gq[:, 2:3, :], 2)
-        quantize_w("q2", 1)
-        dz_slot[1] = quantize("slot1", g1, E5M2)
-        dw_chunk(SSSS, "dwk0", 0, dz_tok["k"], out_2)()
-        rope_sums(pr, dzq[:, 2:3, :])
-        dx_banks(SSSS, 0, (1,))
-        dw_chunk(SSSS, "dwk1", 1, dz_tok["k"], out_2)()
-        g2 = slot_turn(2)
-        dx_banks(SSSS, 1, (0, 1))
-
-        pr = rope_products("s3a", gq[:, 3:4, :N], 3)
-        rope_sums(pr, dzq[:, 3:4, :N])
-        pr = rope_products("s3b", gq[:, 3:4, N:], 3)
-        q0_tok = group_tokens(V, "q0_tok", dzq[:, :, :N])
-        dz_slot[2] = quantize("slot2", g2, E5M2)
         dz_tok["q0"] = quantize("q0_tok", q0_tok, E5M2)
+        quantize_w("q2", 1)
+        dx_banks(SSSS, 0, (0,))
         dw_chunk(SSSS, "dwk2", 2, dz_tok["k"], out_2)()
-        rope_sums(pr, dzq[:, 3:4, N:])
-        dx_banks(SSSS, 2, (0, 1))
+        turn_w("v", 2)
+        dw_chunk(SSSS, "dwv2", 2, dz_tok["v"], out_3)()
+        dx_banks(SSSS, 0, (1,))
+
+        b = sin_product("s1", psum_tables, gq[:, 1:2, N:], 1)
+        rope_sum(G, a, b, dzq[:, 1:2, N:])
+        a = cos_product("s2", psum_tables, gq[:, 2:3, N:], 2)
+        b = sin_product("s2", psum_tables, gq[:, 2:3, N:], 2)
+        rope_sum(G, a, b, dzq[:, 2:3, N:])
+        a = cos_product("s3", psum_tables, gq[:, 3:4, N:], 3)
+        b = sin_product("s3", psum_tables, gq[:, 3:4, N:], 3)
+        rope_sum(G, a, b, dzq[:, 3:4, N:])
+        turn_w("k", 2)
         dw_chunk(SSSS, "dwq00", 0, dz_tok["q0"], out_1[:, :N])()
-        turn_w("v", 2, (V, V))
-        q1_tok = group_tokens(V, "q1_tok", dzq[:, :, N : 2 * N])
-        quantize_w("v", 2)
-        turn_w("k", 2, (V, V))
-        dz_tok["q1"] = quantize("q1_tok", q1_tok, E5M2)
-        dw_chunk(SSSS, "dwq01", 1, dz_tok["q0"], out_1[:, :N])()
-        q2_tok = group_tokens(V, "q2_tok", dzq[:, :, 2 * N :])
-        quantize_w("k", 2)
+        g1 = slot_turn(1)
         turn_w("q0", 2, (V, V))
-        dz_tok["q2"] = quantize("q2_tok", q2_tok, E5M2)
+        g2 = slot_turn(2, (V, V))
+        dw_chunk(SSSS, "dwq01", 1, dz_tok["q0"], out_1[:, :N])()
         dw_chunk(SSSS, "dwq02", 2, dz_tok["q0"], out_1[:, :N])()
-        turn_w("q1", 2, (V, V))
+        dz_slot[1] = quantize("slot1", g1, E5M2)
+        q1_tok = group_tokens(V, "q1_tok", dzq[:, :, N : 2 * N], True)
+        dz_slot[2] = quantize("slot2", g2, E5M2)
+        q2_tok = group_tokens(V, "q2_tok", dzq[:, :, 2 * N :], True)
+        dz_tok["q1"] = quantize("q1_tok", q1_tok, E5M2)
+        dz_tok["q2"] = quantize("q2_tok", q2_tok, E5M2)
+        quantize_w("v", 2)
+        quantize_w("k", 2)
         quantize_w("q0", 2)
+        dx_banks(SSSS, 1, (0, 1))
+        dx_banks(SSSS, 2, (0, 1))
         dw_pair(SSSS, 0, 0)
+        turn_w("q1", 2, (V, V))
+        dw_pair(SSSS, 0, 1)
         turn_w("q2", 2, (V, V))
         quantize_w("q1", 2)
         g3 = slot_turn(3, (V, V))
         quantize_w("q2", 2)
-        dw_pair(SSSS, 0, 1)
+        dw_pair(SSSS, 1, 0)
         dz_slot[3] = quantize("slot3", g3, E5M2)
-        dx_banks(VS, 0, (2,))
-        dw_pair(SV, 1, 0)
-        dx_banks(VS, 1, (2,))
         dw_pair(SV, 1, 1)
-        dx_banks(VS, 2, (2,))
+        dx_banks(VS, 0, (2,))
         dw_pair(SV, 2, 0)
-        dx_banks(VS, 3, (0, 1, 2))
+        dx_banks(VS, 1, (2,))
         dw_pair(SV, 2, 1)
+        dx_banks(VS, 2, (2,))
+        dx_banks(SV, 3, (0,))
+        dx_banks(VS, 3, (1,))
+        dx_banks(SV, 3, (2,))

@@ -3,9 +3,9 @@ from contextlib import ExitStack
 import concourse.mybir as mybir
 from concourse.masks import make_identity
 
-T, E, D2 = 512, 1536, 64
-JQ, JK = 1536, 512
-FLOPS = 2 * 2 * T * E * (JQ + 2 * JK)
+TOKENS, MODEL, HALF_HEAD = 512, 1536, 64
+Q_FEATURES, KV_FEATURES = 1536, 512
+FLOPS = 2 * 2 * TOKENS * MODEL * (Q_FEATURES + 2 * KV_FEATURES)
 
 F32 = mybir.dt.float32
 BF16 = mybir.dt.bfloat16
@@ -18,7 +18,14 @@ ALU = mybir.AluOpType
 P = 128
 PACK = 4
 N = 512
-CHUNKS = E // N
+TABLE = PACK * HALF_HEAD
+COS, SIN, MINUS_SIN = 0, 1, 2
+
+ROTATING_BANKS = 7
+WIDE_BUFS = 4
+NARROW_BUFS = 4
+GROUPED_BUFS = 5
+STAGE_BUFS = 5
 
 
 def tile_llamaattentionfused_pa_v_kernel(
@@ -27,52 +34,151 @@ def tile_llamaattentionfused_pa_v_kernel(
     nc = tc.nc
     with ExitStack() as ctx:
         sb = ctx.enter_context(tc.tile_pool(name="sb", bufs=1))
-        psum = ctx.enter_context(tc.psum_pool(name="psum", bufs=7))
+        psum = ctx.enter_context(tc.psum_pool(name="psum", bufs=ROTATING_BANKS))
         psum_keep = ctx.enter_context(tc.psum_pool(name="psum_keep", bufs=1))
         ctx.enter_context(tc.manual_schedule())
 
         ident = sb.tile([P, P], F32, name="ident")
         make_identity(nc, ident[:])
 
-        def copy(engine, out, in_):
-            if engine == "vector":
-                nc.vector.tensor_copy(out=out, in_=in_)
+        scalar, vector = nc.scalar.copy, nc.vector.tensor_copy
+        x_mx, dz_tokens, dz_row, w_mx = {}, {}, {}, {}
+        w_raw, w_grouped, stages = {}, {}, {}
+
+
+        def bf16_tile(name, width, tag, bufs):
+            tile = sb.tile([P, width], BF16, name=name, tag=tag, bufs=bufs, align_bytes=64)
+            return tile
+
+        def grouped_tile(name, in_narrow=False):
+            if in_narrow:
+                return bf16_tile(name, PACK * N, "narrow", NARROW_BUFS)
+            return bf16_tile(name, PACK * N, "grouped", GROUPED_BUFS)
+
+        def four_rows(tile):
+            return tile[:].rearrange("p (j c) -> p j c", j=PACK)
+
+        def load(name, src):
+            width = src.shape[1]
+            if width == PACK * N:
+                tile = bf16_tile(name, width, "narrow", NARROW_BUFS)
             else:
-                nc.scalar.copy(out=out, in_=in_)
+                tile = bf16_tile(name, width, "wide", WIDE_BUFS)
+            nc.sync.dma_start(out=tile[:], in_=src)
+            return four_rows(tile)
 
-        def load(name, src, tag, bufs):
-            t = sb.tile([P, src.shape[1]], BF16, name=name, tag=tag, bufs=bufs, align_bytes=64)
-            nc.sync.dma_start(out=t[:], in_=src)
-            return t[:].rearrange("p (j c) -> p j c", j=PACK)
+        def load_gradient(name, grad):
+            return load(name, grad.rearrange("b (p j) h d -> p (b j h d)", j=PACK))
 
-        def load_wide(name, src):
-            return load(name, src, "wide", 4)
+        def load_weight(name, w, third):
+            return load(name + str(third), w[N * third : N * (third + 1), :].rearrange("(p r) c -> p (r c)", r=PACK))
 
-        def load_narrow(name, src):
-            return load(name, src, "narrow", 4)
+        def load_wv(third):
+            w_raw["v", third] = load_weight("wv", wv, third)
 
-        def weight_rows(w, n):
-            return w[N * n : N * (n + 1), :].rearrange("(p r) c -> p (r c)", r=PACK)
+        def load_wk(third):
+            w_raw["k", third] = load_weight("wk", wk, third)
 
-        def grouped_tile(name, width=PACK * N):
-            t = sb.tile([P, width], BF16, name=name, tag="grouped", bufs=5, align_bytes=64)
-            return t
+        def load_wq(third):
+            rows = load_weight("wq", wq, third)
+            for i in range(Q_FEATURES // N):
+                w_raw["q%d" % i, third] = rows[:, :, N * i : N * (i + 1)]
 
-        def spare_tile(name):
-            t = sb.tile([P, PACK * N], BF16, name=name, tag="narrow", bufs=4, align_bytes=64)
-            return t
+
+        def table_view(tables, kind, j0, rows, repeats):
+            one = tables.rearrange("p (k j i) -> p k j i", k=3, i=HALF_HEAD)[:, kind, j0 : j0 + rows, :]
+            return one.unsqueeze(2).to_broadcast([P, rows, repeats, HALF_HEAD])
+
+        def cos_product(name, tables, g, j0):
+            rows, width = g.shape[1], g.shape[2]
+            product = sb.tile([P, rows * width], F32, name=name + "_cos", tag="cos_product", bufs=2)
+            nc.vector.tensor_tensor(
+                out=product[:].rearrange("p (j h i) -> p j h i", j=rows, i=HALF_HEAD),
+                in0=g.rearrange("p j (h i) -> p j h i", i=HALF_HEAD),
+                in1=table_view(tables, COS, j0, rows, width // HALF_HEAD),
+                op=ALU.mult,
+            )
+            return product
+
+        def sin_product(name, tables, g, j0):
+            rows, width = g.shape[1], g.shape[2]
+            product = sb.tile([P, rows * width], F32, name=name + "_sin", tag="sin_product", bufs=2)
+            halves_out = product[:].rearrange("p (j h two i) -> p j h two i", j=rows, two=2, i=HALF_HEAD)
+            halves_in = g.rearrange("p j (h two i) -> p j h two i", two=2, i=HALF_HEAD)
+            for half, kind in enumerate((SIN, MINUS_SIN)):
+                nc.vector.tensor_tensor(
+                    out=halves_out[:, :, :, half, :],
+                    in0=halves_in[:, :, :, 1 - half, :],
+                    in1=table_view(tables, kind, j0, rows, width // (2 * HALF_HEAD)),
+                    op=ALU.mult,
+                )
+            return product
+
+        def rope_sum(engine, with_cos, with_sin, dz):
+            rows = dz.shape[1]
+            engine.tensor_tensor(
+                out=dz,
+                in0=with_cos[:].rearrange("p (j c) -> p j c", j=rows),
+                in1=with_sin[:].rearrange("p (j c) -> p j c", j=rows),
+                op=ALU.add,
+            )
+
 
         def quantize(name, grouped, fmt):
-            width = grouped.shape[1] // PACK
-            codes = sb.tile([P, width], U32, name=name + "_codes", align_bytes=64)
-            scales = sb.tile([P, width], U8, name=name + "_scales", align_bytes=64)
+            codes = sb.tile([P, N], U32, name=name + "_codes", align_bytes=64)
+            scales = sb.tile([P, N], U8, name=name + "_scales", align_bytes=64)
             nc.vector.quantize_mx(out=codes[:].bitcast(fmt), scales=scales[:], in_=grouped[:])
             return codes, scales, fmt
 
-        def matmul(out, stationary, col, moving, start, stop):
-            cols = slice(col, col + P)
+        def group_tokens(copy, name, rows, in_narrow=False):
+            grouped = grouped_tile(name, in_narrow)
+            copy(
+                out=grouped[:].rearrange("p (c i j) -> p c j i", i=4, j=PACK),
+                in_=rows.rearrange("p j (c i) -> p c j i", i=4),
+            )
+            return grouped
+
+        def group_x(copy, third):
+            grouped = grouped_tile("x_grouped%d" % third)
+            copy(
+                out=grouped[:].rearrange("p (r m j) -> p m j r", r=PACK, j=PACK),
+                in_=x_rows[:, :, N * third : N * (third + 1)].rearrange("p j (m r) -> p m j r", r=PACK),
+            )
+            return grouped
+
+        def turn(copies, name, sources, in_narrow=False):
+            grouped = grouped_tile(name, in_narrow)
+            banks = []
+            for half in range(2):
+                bank = psum.tile([P, 2, 2, P], F32, name="%s_bank%d" % (name, half), tag="bank")
+                for s in range(2):
+                    words = sources[2 * half + s].bitcast(F32)
+                    for u in range(2):
+                        nc.tensor.transpose(bank[:, s, u, :], words[:, u::2], ident[:])
+                banks.append(bank)
+            for half, bank in enumerate(banks):
+                copies[half](
+                    out=grouped[:].bitcast(F32)[:, N * half : N * (half + 1)].rearrange("p (s r u) -> p s r u", s=2, u=2),
+                    in_=bank[:].rearrange("p s u r -> p s r u"),
+                )
+            return grouped
+
+        def turn_w(part, third, copies=(scalar, scalar)):
+            raw = w_raw[part, third]
+            w_grouped[part, third] = turn(copies, "w%s%d_grouped" % (part, third), [raw[:, r, :] for r in range(PACK)])
+
+        def quantize_w(part, third):
+            w_mx[part, third] = quantize("w%s%d" % (part, third), w_grouped[part, third], E4M3)
+
+        def turn_row(j, copies=(scalar, scalar), in_narrow=False):
+            sources = [dk[:, j, :]] + [dq[:, j, N * i : N * (i + 1)] for i in range(Q_FEATURES // N)]
+            return turn(copies, "row%d_grouped" % j, sources, in_narrow)
+
+
+        def matmul(bank, stationary, block, moving, start, stop):
+            cols = slice(P * block, P * (block + 1))
             nc.tensor.matmul_mx(
-                out=out,
+                out=bank[:],
                 lhsT=stationary[0][:, cols].bitcast(stationary[2]),
                 lhsT_scale=stationary[1][:, cols],
                 rhs=moving[0][:].bitcast(moving[2]),
@@ -81,299 +187,206 @@ def tile_llamaattentionfused_pa_v_kernel(
                 stop=stop,
             )
 
-        def table_view(tables, kind, j0, slots, reps):
-            rows = tables.rearrange("p (k j i) -> p k j i", k=3, i=D2)[:, kind, j0 : j0 + slots, :]
-            return rows.unsqueeze(2).to_broadcast([P, slots, reps, D2])
-
-        def cos_product(name, tables, g, j0):
-            slots, width = g.shape[1], g.shape[2]
-            prod = sb.tile([P, slots * width], F32, name=name + "_cos", tag="prod_cos", bufs=2)
-            nc.vector.tensor_tensor(
-                out=prod[:].rearrange("p (j h i) -> p j h i", j=slots, i=D2),
-                in0=g.rearrange("p j (h i) -> p j h i", i=D2),
-                in1=table_view(tables, 0, j0, slots, width // D2),
-                op=ALU.mult,
-            )
-            return prod
-
-        def sin_product(name, tables, g, j0):
-            slots, width = g.shape[1], g.shape[2]
-            prod = sb.tile([P, slots * width], F32, name=name + "_sin", tag="prod_sin", bufs=2)
-            for half in range(2):
-                nc.vector.tensor_tensor(
-                    out=prod[:].rearrange("p (j h two i) -> p j h two i", j=slots, two=2, i=D2)[:, :, :, half, :],
-                    in0=g.rearrange("p j (h two i) -> p j h two i", two=2, i=D2)[:, :, :, 1 - half, :],
-                    in1=table_view(tables, 1 + half, j0, slots, width // (2 * D2)),
-                    op=ALU.mult,
-                )
-            return prod
-
-        def rope_sum(engine, a, b, dz):
-            slots = dz.shape[1]
-            engine.tensor_tensor(
-                out=dz,
-                in0=a[:].rearrange("p (j c) -> p j c", j=slots),
-                in1=b[:].rearrange("p (j c) -> p j c", j=slots),
-                op=ALU.add,
-            )
-
-        def group_tokens(engine, name, rows, late=False):
-            grouped = spare_tile(name) if late else grouped_tile(name)
-            copy(
-                engine,
-                grouped[:].rearrange("p (c i j) -> p c j i", i=4, j=PACK),
-                rows.rearrange("p j (c i) -> p c j i", i=4),
-            )
-            return grouped
-
-        def group_x(engine, n):
-            grouped = grouped_tile("x_grouped%d" % n)
-            copy(
-                engine,
-                grouped[:].rearrange("p (r m j) -> p m j r", r=PACK, j=PACK),
-                x_rows[:, :, N * n : N * (n + 1)].rearrange("p j (m r) -> p m j r", r=PACK),
-            )
-            return grouped
-
-        def transpose_pair(engine, name, sources, grouped, half):
-            bank = psum.tile([P, 2, 2, P], F32, name=name, tag="bank")
-            for s, src in enumerate(sources):
-                words = src.bitcast(F32)
-                for u in range(2):
-                    nc.tensor.transpose(bank[:, s, u, :], words[:, u::2], ident[:])
-            dst = grouped[:].bitcast(F32)[:, N * half : N * (half + 1)]
-            return lambda: copy(engine, dst.rearrange("p (s r u) -> p s r u", s=2, u=2), bank[:].rearrange("p s u r -> p s r u"))
-
-        def transpose_rows(engines, name, rows):
-            grouped = grouped_tile(name)
-            outs = [
-                transpose_pair(engines[h], name + "_bank%d" % h, [rows[:, 2 * h, :], rows[:, 2 * h + 1, :]], grouped, h)
-                for h in range(2)
-            ]
-            for o in outs:
-                o()
-            return grouped
-
         def stage_tile(name, width):
-            t = sb.tile([P, width], F32, name=name, tag="stage", bufs=5)
-            return t
+            tile = sb.tile([P, width], F32, name=name, tag="stage", bufs=STAGE_BUFS)
+            return tile
 
-        def dw_bank(engine, name, n, r, dz, dst):
+        def dw_bank(copy, name, part, third, r, dst):
             bank = psum.tile([P, N], F32, name=name, tag="bank")
-            matmul(bank[:], x_mx[n], P * r, dz, True, True)
-            copy(engine, dst, bank[:])
+            matmul(bank, x_mx[third], r, dz_tokens[part], True, True)
+            copy(out=dst, in_=bank[:])
 
-        def dw_chunk(engines, name, n, dz, out_cols):
-            stage = stage_tile(name, PACK * N)
-            for r in range(PACK):
-                dw_bank(engines[r], name + "_bank%d" % r, n, r, dz, stage[:, N * r : N * (r + 1)])
-            return lambda: nc.sync.dma_start(
-                out=out_cols[N * n : N * (n + 1), :].rearrange("(m r) c -> m r c", r=PACK),
-                in_=stage[:].rearrange("p (r c) -> p r c", r=PACK),
-            )
+        def dw_half(part, third, half):
+            name = "dw%s%d" % (part, third)
+            if half == 0:
+                stages[name] = stage_tile(name, PACK * N)
+            for r in (2 * half, 2 * half + 1):
+                dw_bank(scalar, "%s_bank%d" % (name, r), part, third, r, stages[name][:, N * r : N * (r + 1)])
+            if half == 1:
+                columns = {"k": out_2, "v": out_3, "q0": out_1[:, :N]}[part]
+                nc.sync.dma_start(
+                    out=columns[N * third : N * (third + 1), :].rearrange("(m r) c -> m r c", r=PACK),
+                    in_=four_rows(stages[name]),
+                )
 
-        def dw_pair(engines, n, half):
-            name = "dwq_%d_%d" % (n, half)
+        def dw_q12(copy_q2, third, half):
+            name = "dwq12_%d_%d" % (third, half)
             stage = stage_tile(name, PACK * N)
             for s in range(2):
-                for c in range(2):
+                for c, (part, copy) in enumerate((("q1", scalar), ("q2", copy_q2))):
                     i = 2 * s + c
-                    dw_bank(engines[i], name + "_bank%d" % i, n, 2 * half + s, dz_tok["q%d" % (c + 1)], stage[:, N * i : N * (i + 1)])
-            rows = out_1[N * n : N * (n + 1), N:].rearrange("(m r) c -> m r c", r=PACK)
-            nc.sync.dma_start(out=rows[:, 2 * half : 2 * half + 2, :], in_=stage[:].rearrange("p (r c) -> p r c", r=2))
+                    dw_bank(copy, "%s_bank%d" % (name, i), part, third, 2 * half + s, stage[:, N * i : N * (i + 1)])
+            rows = out_1[N * third : N * (third + 1), N:].rearrange("(m r) c -> m r c", r=PACK)
+            nc.sync.dma_start(
+                out=rows[:, 2 * half : 2 * half + 2, :], in_=stage[:].rearrange("p (r c) -> p r c", r=2)
+            )
 
-        def dwq_rows(engines, n, r):
-            name = "dwq_%d_%d" % (n, r)
-            stage = stage_tile(name, JQ)
-            for c in range(3):
-                dw_bank(engines[c], name + "_bank%d" % c, n, r, dz_tok["q%d" % c], stage[:, N * c : N * (c + 1)])
-            rows = out_1[N * n : N * (n + 1), :].rearrange("(m r) c -> m r c", r=PACK)
-            nc.sync.dma_start(out=rows[:, r, :], in_=stage[:])
-
-        def dx_banks(engines, j, ns):
-            stage = stage_tile("dx%d_%d" % (j, ns[0]), N * len(ns))
-            for s, n in enumerate(ns):
-                bank = psum.tile([P, N], F32, name="dx%d_bank%d" % (j, n), tag="bank")
-                terms = [(dz_feat["v"], P * j, w_mx["v", n])]
-                terms += [(dz_slot[j], P * i, w_mx[c, n]) for i, c in enumerate(("k", "q0", "q1", "q2"))]
-                for i, (stationary, col, moving) in enumerate(terms):
-                    matmul(bank[:], stationary, col, moving, i == 0, i == len(terms) - 1)
-                copy(
-                    engines[s],
-                    stage[:, N * s : N * (s + 1)].rearrange("p (m r) -> p m r", r=PACK),
-                    bank[:].rearrange("p (r m) -> p m r", r=PACK),
-                )
-            rows = out_0.rearrange("b (p j) e -> p (b j) e", j=PACK)
-            nc.sync.dma_start(out=rows[:, j, N * ns[0] : N * (ns[-1] + 1)], in_=stage[:])
-
-        def token_rows(g):
-            return g.rearrange("b (p j) h d -> p (b j h d)", j=PACK)
-
-        S, V = "scalar", "vector"
-        x_mx, dz_tok, dz_feat, dz_slot, w_mx, w_rows, w_grouped = {}, {}, {}, {}, {}, {}, {}
-
-        def load_weights(n):
-            w_rows["v", n] = load_narrow("wv%d" % n, weight_rows(wv, n))
-            w_rows["k", n] = load_narrow("wk%d" % n, weight_rows(wk, n))
-            load_wq(n)
-
-        def load_wq(n):
-            rows = load_wide("wq%d" % n, weight_rows(wq, n))
-            for i in range(3):
-                w_rows["q%d" % i, n] = rows[:, :, N * i : N * (i + 1)]
-
-        def turn_w(c, n, engines=(S, S)):
-            w_grouped[c, n] = transpose_rows(engines, "w%s%d_grouped" % (c, n), w_rows[c, n])
-
-        def quantize_w(c, n):
-            w_mx[c, n] = quantize("w%s%d" % (c, n), w_grouped[c, n], E4M3)
+        def dx_bank(copy, j, third, stored_together):
+            first, last = stored_together[0], stored_together[-1]
+            name = "dx%d_%d" % (j, first)
+            if third == first:
+                stages[name] = stage_tile(name, N * len(stored_together))
+            bank = psum.tile([P, N], F32, name="dx%d_bank%d" % (j, third), tag="bank")
+            passes = [(dv_features, j, "v")] + [(dz_row[j], i, part) for i, part in enumerate(("k", "q0", "q1", "q2"))]
+            for i, (stationary, block, part) in enumerate(passes):
+                matmul(bank, stationary, block, w_mx[part, third], i == 0, i == len(passes) - 1)
+            place = third - first
+            copy(
+                out=stages[name][:, N * place : N * (place + 1)].rearrange("p (m r) -> p m r", r=PACK),
+                in_=bank[:].rearrange("p (r m) -> p m r", r=PACK),
+            )
+            if third == last:
+                rows = out_0.rearrange("b (p j) e -> p (b j) e", j=PACK)
+                nc.sync.dma_start(out=rows[:, j, N * first : N * (last + 1)], in_=stages[name][:])
 
 
-        TAB = PACK * D2
-        tables = sb.tile([P, 3 * TAB], BF16, name="tables", align_bytes=64)
-        nc.sync.dma_start(out=tables[:, :TAB], in_=freqs_cos.rearrange("(p j) i -> p (j i)", j=PACK))
-        nc.sync.dma_start(out=tables[:, TAB : 2 * TAB], in_=freqs_sin.rearrange("(p j) i -> p (j i)", j=PACK))
-        gk = load_narrow("gk", token_rows(grad_1))
-        gv = load_narrow("gv", token_rows(grad_2))
-        w_rows["k", 0] = load_narrow("wk0", weight_rows(wk, 0))
-        w_rows["v", 0] = load_narrow("wv0", weight_rows(wv, 0))
-        x_rows = load_wide("x", x.rearrange("b (p j) e -> p (b j e)", j=PACK))
+        tables = sb.tile([P, 3 * TABLE], BF16, name="tables", align_bytes=64)
+        nc.sync.dma_start(out=tables[:, :TABLE], in_=freqs_cos.rearrange("(p j) i -> p (j i)", j=PACK))
+        nc.sync.dma_start(out=tables[:, TABLE : 2 * TABLE], in_=freqs_sin.rearrange("(p j) i -> p (j i)", j=PACK))
+        gk = load_gradient("gk", grad_1)
+        dv = load_gradient("dv", grad_2)
+        x_rows = load("x", x.rearrange("b (p j) e -> p (b j e)", j=PACK))
+        load_wv(0)
+        load_wk(0)
         load_wq(0)
 
-        SSSS = (S, S, S, S)
-        SV = (S, V, S, V)
-        VS = (V, S, V, S)
-        dzk_tile = sb.tile([P, PACK * N], BF16, name="dzk", align_bytes=64)
-        dzk = dzk_tile[:].rearrange("p (j c) -> p j c", j=PACK)
-        dzq_tile = sb.tile([P, PACK * JQ], BF16, name="dzq", align_bytes=64)
-        dzq = dzq_tile[:].rearrange("p (j c) -> p j c", j=PACK)
+        dk_tile = sb.tile([P, PACK * KV_FEATURES], BF16, name="dk", align_bytes=64)
+        dq_tile = sb.tile([P, PACK * Q_FEATURES], BF16, name="dq", align_bytes=64)
+        dk, dq = four_rows(dk_tile), four_rows(dq_tile)
 
-        def slot_turn(j, engines=(S, S)):
-            grouped = grouped_tile("slot%d_grouped" % j)
-            a = transpose_pair(engines[0], "slot%d_a" % j, [dzk[:, j, :], dzq[:, j, :N]], grouped, 0)
-            b = transpose_pair(engines[1], "slot%d_b" % j, [dzq[:, j, N : 2 * N], dzq[:, j, 2 * N :]], grouped, 1)
-            a()
-            b()
-            return grouped
-
-        nc.vector.tensor_scalar(out=tables[:, 2 * TAB :], in0=tables[:, TAB : 2 * TAB], scalar1=-1.0, scalar2=None, op0=ALU.mult)
-        turned_bank = psum.tile([P, 3, P], F32, name="turned_bank", tag="bank")
-        turned = sb.tile([P, 3, P], F32, name="turned")
+        nc.vector.tensor_scalar(
+            out=tables[:, 2 * TABLE :], in0=tables[:, TABLE : 2 * TABLE], scalar1=-1.0, scalar2=None, op0=ALU.mult
+        )
+        transposed_bank = psum.tile([P, 3, P], F32, name="transposed_bank", tag="bank")
+        transposed = sb.tile([P, 3, P], F32, name="transposed")
         table_bank = psum_keep.tile([P, 3 * P], F32, name="table_bank")
-        for kind in range(3):
-            nc.tensor.transpose(turned_bank[:, kind, :], tables[:].bitcast(F32)[:, P * kind : P * (kind + 1)], ident[:])
-        nc.scalar.copy(out=turned[:], in_=turned_bank[:])
-        for kind in range(3):
-            nc.tensor.transpose(table_bank[:, P * kind : P * (kind + 1)], turned[:, kind, :], ident[:])
+        for kind in (COS, SIN, MINUS_SIN):
+            nc.tensor.transpose(
+                transposed_bank[:, kind, :], tables[:].bitcast(F32)[:, P * kind : P * (kind + 1)], ident[:]
+            )
+        nc.scalar.copy(out=transposed[:], in_=transposed_bank[:])
+        for kind in (COS, SIN, MINUS_SIN):
+            nc.tensor.transpose(table_bank[:, P * kind : P * (kind + 1)], transposed[:, kind, :], ident[:])
         psum_tables = table_bank[:].bitcast(BF16)
 
-        G = nc.gpsimd
-        a = cos_product("k0", tables[:], gk[:, 0:2, :], 0)
-        b = sin_product("k0", tables[:], gk[:, 0:2, :], 0)
-        a1 = cos_product("k1", tables[:], gk[:, 2:4, :], 2)
-        rope_sum(nc.vector, a, b, dzk[:, 0:2, :])
-        v_tok = group_tokens(S, "v_tok", gv)
-        v_feat = transpose_rows((S, S), "v_feat", gv)
-        dz_tok["v"] = quantize("v_tok", v_tok, E5M2)
-        b1 = sin_product("k1", tables[:], gk[:, 2:4, :], 2)
-        turn_w("k", 0)
-        turn_w("v", 0)
-        dz_feat["v"] = quantize("v_feat", v_feat, E5M2)
-        rope_sum(nc.vector, a1, b1, dzk[:, 2:4, :])
-        quantize_w("k", 0)
-        w_rows["v", 1] = load_narrow("wv1", weight_rows(wv, 1))
-        w_rows["k", 1] = load_narrow("wk1", weight_rows(wk, 1))
-        gq = load_wide("gq", token_rows(grad_0))
+        gq = load_gradient("gq", grad_0)
+        with_cos = cos_product("k01", tables[:], gk[:, 0:2, :], 0)
+        with_sin = sin_product("k01", tables[:], gk[:, 0:2, :], 0)
+        rope_sum(nc.gpsimd, with_cos, with_sin, dk[:, 0:2, :])
+        with_cos = cos_product("k23", psum_tables, gk[:, 2:4, :], 2)
+        with_sin = sin_product("k23", psum_tables, gk[:, 2:4, :], 2)
+        load_wv(1)
+        dv_by_tokens = group_tokens(scalar, "dv_by_tokens", dv)
+        dv_by_features = turn((scalar, scalar), "dv_by_features", [dv[:, j, :] for j in range(PACK)])
+        load_wk(1)
         load_wq(1)
-        x0 = group_x(S, 0)
-        k_tok = group_tokens(V, "k_tok", dzk)
+        x0_grouped = group_x(vector, 0)
+        x1_grouped = group_x(scalar, 1)
+        dz_tokens["v"] = quantize("dv_tokens", dv_by_tokens, E5M2)
+        x_mx[0] = quantize("x0", x0_grouped, E4M3)
+        rope_sum(nc.vector, with_cos, with_sin, dk[:, 2:4, :])
+        turn_w("v", 0)
+        turn_w("k", 0)
+        dw_half("v", 0, 0)
+        dw_half("v", 0, 1)
+        x_mx[1] = quantize("x1", x1_grouped, E4M3)
+        dv_features = quantize("dv_features", dv_by_features, E5M2)
+        x2_grouped = group_x(vector, 2)
         quantize_w("v", 0)
-        dz_tok["k"] = quantize("k_tok", k_tok, E5M2)
-        x_mx[0] = quantize("x0", x0, E4M3)
-        x1 = group_x(S, 1)
-        x2 = group_x(V, 2)
-        load_weights(2)
-        x_mx[1] = quantize("x1", x1, E4M3)
+        x_mx[2] = quantize("x2", x2_grouped, E4M3)
+        dk_by_tokens = group_tokens(vector, "dk_by_tokens", dk)
+        quantize_w("k", 0)
+
         turn_w("q0", 0)
+        dw_half("v", 1, 0)
+        dz_tokens["k"] = quantize("dk_tokens", dk_by_tokens, E5M2)
         turn_w("q1", 0)
-        turn_w("q2", 0)
-        x_mx[2] = quantize("x2", x2, E4M3)
+        dw_half("v", 1, 1)
+        load_wv(2)
+        load_wk(2)
+        load_wq(2)
+        with_cos = cos_product("row0", psum_tables, gq[:, 0:1, :], 0)
         quantize_w("q0", 0)
+        turn_w("q2", 0, (vector, vector))
+        dw_half("v", 2, 0)
         quantize_w("q1", 0)
-        dw_chunk(SSSS, "dwk0", 0, dz_tok["k"], out_2)()
         turn_w("v", 1)
-        turn_w("k", 1)
-        dw_chunk(SSSS, "dwv0", 0, dz_tok["v"], out_3)()
-
-        a = cos_product("s0", psum_tables, gq[:, 0:1, :], 0)
+        dw_half("v", 2, 1)
         quantize_w("q2", 0)
-        b = sin_product("s0", psum_tables, gq[:, 0:1, :], 0)
-        rope_sum(G, a, b, dzq[:, 0:1, :])
-        a = cos_product("q0", psum_tables, gq[:, 1:4, :N], 1)
-        b = sin_product("q0", psum_tables, gq[:, 1:4, :N], 1)
-        rope_sum(G, a, b, dzq[:, 1:4, :N])
-        a = cos_product("s1", psum_tables, gq[:, 1:2, N:], 1)
-        dw_chunk(SSSS, "dwk1", 1, dz_tok["k"], out_2)()
-        turn_w("q0", 1, (V, V))
-        g0 = slot_turn(0)
-        turn_w("q1", 1, (V, V))
-        dw_chunk(SSSS, "dwv1", 1, dz_tok["v"], out_3)()
-        dz_slot[0] = quantize("slot0", g0, E5M2)
-        quantize_w("v", 1)
+        with_sin = sin_product("row0", psum_tables, gq[:, 0:1, :], 0)
+        rope_sum(nc.gpsimd, with_cos, with_sin, dq[:, 0:1, :])
+        with_cos = cos_product("q0_rest", psum_tables, gq[:, 1:4, :N], 1)
+        with_sin = sin_product("q0_rest", psum_tables, gq[:, 1:4, :N], 1)
+        rope_sum(nc.gpsimd, with_cos, with_sin, dq[:, 1:4, :N])
+        turn_w("k", 1)
+        dw_half("k", 0, 0)
+        dw_half("k", 0, 1)
+        turn_w("q0", 1)
+        dw_half("k", 1, 0)
+        turn_w("q1", 1, (vector, vector))
+        with_cos = cos_product("row1", psum_tables, gq[:, 1:2, N:], 1)
+        dw_half("k", 1, 1)
+        row0_grouped = turn_row(0, (vector, vector), in_narrow=True)
+        dw_half("k", 2, 0)
+        dz_row[0] = quantize("row0", row0_grouped, E5M2)
         turn_w("q2", 1)
-        quantize_w("k", 1)
-        q0_tok = group_tokens(V, "q0_tok", dzq[:, :, :N])
-        quantize_w("q0", 1)
-        quantize_w("q1", 1)
-        dz_tok["q0"] = quantize("q0_tok", q0_tok, E5M2)
-        quantize_w("q2", 1)
-        dx_banks(SSSS, 0, (0,))
-        dw_chunk(SSSS, "dwk2", 2, dz_tok["k"], out_2)()
-        turn_w("v", 2)
-        dw_chunk(SSSS, "dwv2", 2, dz_tok["v"], out_3)()
-        dx_banks(SSSS, 0, (1,))
+        dw_half("k", 2, 1)
 
-        b = sin_product("s1", psum_tables, gq[:, 1:2, N:], 1)
-        rope_sum(G, a, b, dzq[:, 1:2, N:])
-        a = cos_product("s2", psum_tables, gq[:, 2:3, N:], 2)
-        b = sin_product("s2", psum_tables, gq[:, 2:3, N:], 2)
-        rope_sum(G, a, b, dzq[:, 2:3, N:])
-        a = cos_product("s3", psum_tables, gq[:, 3:4, N:], 3)
-        b = sin_product("s3", psum_tables, gq[:, 3:4, N:], 3)
-        rope_sum(G, a, b, dzq[:, 3:4, N:])
-        turn_w("k", 2)
-        dw_chunk(SSSS, "dwq00", 0, dz_tok["q0"], out_1[:, :N])()
-        g1 = slot_turn(1)
-        turn_w("q0", 2, (V, V))
-        g2 = slot_turn(2, (V, V))
-        dw_chunk(SSSS, "dwq01", 1, dz_tok["q0"], out_1[:, :N])()
-        dw_chunk(SSSS, "dwq02", 2, dz_tok["q0"], out_1[:, :N])()
-        dz_slot[1] = quantize("slot1", g1, E5M2)
-        q1_tok = group_tokens(V, "q1_tok", dzq[:, :, N : 2 * N], True)
-        dz_slot[2] = quantize("slot2", g2, E5M2)
-        q2_tok = group_tokens(V, "q2_tok", dzq[:, :, 2 * N :], True)
-        dz_tok["q1"] = quantize("q1_tok", q1_tok, E5M2)
-        dz_tok["q2"] = quantize("q2_tok", q2_tok, E5M2)
-        quantize_w("v", 2)
-        quantize_w("k", 2)
-        quantize_w("q0", 2)
-        dx_banks(SSSS, 1, (0, 1))
-        dx_banks(SSSS, 2, (0, 1))
-        dw_pair(SSSS, 0, 0)
-        turn_w("q1", 2, (V, V))
-        dw_pair(SSSS, 0, 1)
-        turn_w("q2", 2, (V, V))
+        q0_by_tokens = group_tokens(vector, "q0_by_tokens", dq[:, :, :N], in_narrow=True)
+        quantize_w("v", 1)
+        dz_tokens["q0"] = quantize("q0_tokens", q0_by_tokens, E5M2)
+        for part in ("k", "q0", "q1", "q2"):
+            quantize_w(part, 1)
+        dx_bank(scalar, 0, 0, (0, 1))
+        turn_w("v", 2)
+        dw_half("q0", 0, 0)
+        dw_half("q0", 0, 1)
+        with_sin = sin_product("row1", psum_tables, gq[:, 1:2, N:], 1)
+        rope_sum(nc.gpsimd, with_cos, with_sin, dq[:, 1:2, N:])
+        with_cos = cos_product("row2", psum_tables, gq[:, 2:3, N:], 2)
+        with_sin = sin_product("row2", psum_tables, gq[:, 2:3, N:], 2)
+        rope_sum(nc.gpsimd, with_cos, with_sin, dq[:, 2:3, N:])
+        turn_w("k", 2, (scalar, vector))
+        with_cos = cos_product("row3", psum_tables, gq[:, 3:4, N:], 3)
+        with_sin = sin_product("row3", psum_tables, gq[:, 3:4, N:], 3)
+        dx_bank(scalar, 0, 1, (0, 1))
+        dw_half("q0", 1, 0)
+        turn_w("q0", 2)
+        dw_half("q0", 1, 1)
+        row1_grouped = turn_row(1, in_narrow=True)
+        rope_sum(nc.vector, with_cos, with_sin, dq[:, 3:4, N:])
+        dz_row[1] = quantize("row1", row1_grouped, E5M2)
+        dw_half("q0", 2, 0)
+        dw_half("q0", 2, 1)
+        row2_grouped = turn_row(2)
+
+        q1_by_tokens = group_tokens(vector, "q1_by_tokens", dq[:, :, N : 2 * N], in_narrow=True)
+        q2_by_tokens = group_tokens(vector, "q2_by_tokens", dq[:, :, 2 * N :], in_narrow=True)
+        dz_tokens["q1"] = quantize("q1_tokens", q1_by_tokens, E5M2)
+        dz_tokens["q2"] = quantize("q2_tokens", q2_by_tokens, E5M2)
+        dz_row[2] = quantize("row2", row2_grouped, E5M2)
+        for part in ("v", "k", "q0"):
+            quantize_w(part, 2)
+        dx_bank(scalar, 1, 0, (0, 1))
+        dx_bank(scalar, 1, 1, (0, 1))
+        turn_w("q1", 2)
+        dw_q12(scalar, 0, 0)
         quantize_w("q1", 2)
-        g3 = slot_turn(3, (V, V))
+        dx_bank(vector, 2, 0, (0,))
+        dw_q12(vector, 0, 1)
+        turn_w("q2", 2, (vector, vector))
+        dw_q12(scalar, 1, 0)
+        row3_grouped = turn_row(3, (vector, vector))
         quantize_w("q2", 2)
-        dw_pair(SSSS, 1, 0)
-        dz_slot[3] = quantize("slot3", g3, E5M2)
-        dw_pair(SV, 1, 1)
-        dx_banks(VS, 0, (2,))
-        dw_pair(SV, 2, 0)
-        dx_banks(VS, 1, (2,))
-        dw_pair(SV, 2, 1)
-        dx_banks(VS, 2, (2,))
-        dx_banks(SV, 3, (0,))
-        dx_banks(VS, 3, (1,))
-        dx_banks(SV, 3, (2,))
+        dw_q12(scalar, 1, 1)
+        dz_row[3] = quantize("row3", row3_grouped, E5M2)
+
+        dx_bank(vector, 0, 2, (2,))
+        dw_q12(vector, 2, 0)
+        dx_bank(vector, 1, 2, (2,))
+        dw_q12(vector, 2, 1)
+        dx_bank(vector, 2, 1, (1, 2))
+        dx_bank(scalar, 2, 2, (1, 2))
+        dx_bank(vector, 3, 0, (0, 1))
+        dx_bank(scalar, 3, 1, (0, 1))
+        dx_bank(vector, 3, 2, (2,))

from contextlib import ExitStack

import concourse.mybir as mybir
from concourse.masks import make_identity

TOKENS, MODEL, HALF_HEAD = 512, 1536, 64
Q_FEATURES, KV_FEATURES = 1536, 512
FLOPS = 2 * 2 * TOKENS * MODEL * (Q_FEATURES + 2 * KV_FEATURES)

F32 = mybir.dt.float32
BF16 = mybir.dt.bfloat16
U32 = mybir.dt.uint32
U8 = mybir.dt.uint8
E4M3 = mybir.dt.float8_e4m3fn_x4
E5M2 = mybir.dt.float8_e5m2_x4
ALU = mybir.AluOpType

P = 128
PACK = 4
N = 512
TABLE = PACK * HALF_HEAD
COS, SIN, MINUS_SIN = 0, 1, 2

ROTATING_BANKS = 7
WIDE_BUFS = 4
NARROW_BUFS = 4
GROUPED_BUFS = 5
STAGE_BUFS = 5


def tile_llamaattentionfused_pa_v_kernel(
    tc, x, wq, wk, wv, freqs_cos, freqs_sin, grad_0, grad_1, grad_2, out_0, out_1, out_2, out_3
):
    nc = tc.nc
    with ExitStack() as ctx:
        sb = ctx.enter_context(tc.tile_pool(name="sb", bufs=1))
        psum = ctx.enter_context(tc.psum_pool(name="psum", bufs=ROTATING_BANKS))
        psum_keep = ctx.enter_context(tc.psum_pool(name="psum_keep", bufs=1))
        ctx.enter_context(tc.manual_schedule())

        ident = sb.tile([P, P], F32, name="ident")
        make_identity(nc, ident[:])

        scalar, vector = nc.scalar.copy, nc.vector.tensor_copy
        x_mx, dz_tokens, dz_row, w_mx = {}, {}, {}, {}
        w_raw, w_grouped, stages = {}, {}, {}


        def bf16_tile(name, width, tag, bufs):
            tile = sb.tile([P, width], BF16, name=name, tag=tag, bufs=bufs, align_bytes=64)
            return tile

        def grouped_tile(name, in_narrow=False):
            if in_narrow:
                return bf16_tile(name, PACK * N, "narrow", NARROW_BUFS)
            return bf16_tile(name, PACK * N, "grouped", GROUPED_BUFS)

        def four_rows(tile):
            return tile[:].rearrange("p (j c) -> p j c", j=PACK)

        def load(name, src):
            width = src.shape[1]
            if width == PACK * N:
                tile = bf16_tile(name, width, "narrow", NARROW_BUFS)
            else:
                tile = bf16_tile(name, width, "wide", WIDE_BUFS)
            nc.sync.dma_start(out=tile[:], in_=src)
            return four_rows(tile)

        def load_gradient(name, grad):
            return load(name, grad.rearrange("b (p j) h d -> p (b j h d)", j=PACK))

        def load_weight(name, w, third):
            return load(name + str(third), w[N * third : N * (third + 1), :].rearrange("(p r) c -> p (r c)", r=PACK))

        def load_wv(third):
            w_raw["v", third] = load_weight("wv", wv, third)

        def load_wk(third):
            w_raw["k", third] = load_weight("wk", wk, third)

        def load_wq(third):
            rows = load_weight("wq", wq, third)
            for i in range(Q_FEATURES // N):
                w_raw["q%d" % i, third] = rows[:, :, N * i : N * (i + 1)]


        def table_view(tables, kind, j0, rows, repeats):
            one = tables.rearrange("p (k j i) -> p k j i", k=3, i=HALF_HEAD)[:, kind, j0 : j0 + rows, :]
            return one.unsqueeze(2).to_broadcast([P, rows, repeats, HALF_HEAD])

        def cos_product(name, tables, g, j0):
            rows, width = g.shape[1], g.shape[2]
            product = sb.tile([P, rows * width], F32, name=name + "_cos", tag="cos_product", bufs=2)
            nc.vector.tensor_tensor(
                out=product[:].rearrange("p (j h i) -> p j h i", j=rows, i=HALF_HEAD),
                in0=g.rearrange("p j (h i) -> p j h i", i=HALF_HEAD),
                in1=table_view(tables, COS, j0, rows, width // HALF_HEAD),
                op=ALU.mult,
            )
            return product

        def sin_product(name, tables, g, j0):
            rows, width = g.shape[1], g.shape[2]
            product = sb.tile([P, rows * width], F32, name=name + "_sin", tag="sin_product", bufs=2)
            halves_out = product[:].rearrange("p (j h two i) -> p j h two i", j=rows, two=2, i=HALF_HEAD)
            halves_in = g.rearrange("p j (h two i) -> p j h two i", two=2, i=HALF_HEAD)
            for half, kind in enumerate((SIN, MINUS_SIN)):
                nc.vector.tensor_tensor(
                    out=halves_out[:, :, :, half, :],
                    in0=halves_in[:, :, :, 1 - half, :],
                    in1=table_view(tables, kind, j0, rows, width // (2 * HALF_HEAD)),
                    op=ALU.mult,
                )
            return product

        def rope_sum(engine, with_cos, with_sin, dz):
            rows = dz.shape[1]
            engine.tensor_tensor(
                out=dz,
                in0=with_cos[:].rearrange("p (j c) -> p j c", j=rows),
                in1=with_sin[:].rearrange("p (j c) -> p j c", j=rows),
                op=ALU.add,
            )


        def quantize(name, grouped, fmt):
            codes = sb.tile([P, N], U32, name=name + "_codes", align_bytes=64)
            scales = sb.tile([P, N], U8, name=name + "_scales", align_bytes=64)
            nc.vector.quantize_mx(out=codes[:].bitcast(fmt), scales=scales[:], in_=grouped[:])
            return codes, scales, fmt

        def group_tokens(copy, name, rows, in_narrow=False):
            grouped = grouped_tile(name, in_narrow)
            copy(
                out=grouped[:].rearrange("p (c i j) -> p c j i", i=4, j=PACK),
                in_=rows.rearrange("p j (c i) -> p c j i", i=4),
            )
            return grouped

        def group_x(copy, third):
            grouped = grouped_tile("x_grouped%d" % third)
            copy(
                out=grouped[:].rearrange("p (r m j) -> p m j r", r=PACK, j=PACK),
                in_=x_rows[:, :, N * third : N * (third + 1)].rearrange("p j (m r) -> p m j r", r=PACK),
            )
            return grouped

        def turn(copies, name, sources, in_narrow=False):
            grouped = grouped_tile(name, in_narrow)
            banks = []
            for half in range(2):
                bank = psum.tile([P, 2, 2, P], F32, name="%s_bank%d" % (name, half), tag="bank")
                for s in range(2):
                    words = sources[2 * half + s].bitcast(F32)
                    for u in range(2):
                        nc.tensor.transpose(bank[:, s, u, :], words[:, u::2], ident[:])
                banks.append(bank)
            for half, bank in enumerate(banks):
                copies[half](
                    out=grouped[:].bitcast(F32)[:, N * half : N * (half + 1)].rearrange("p (s r u) -> p s r u", s=2, u=2),
                    in_=bank[:].rearrange("p s u r -> p s r u"),
                )
            return grouped

        def turn_w(part, third, copies=(scalar, scalar)):
            raw = w_raw[part, third]
            w_grouped[part, third] = turn(copies, "w%s%d_grouped" % (part, third), [raw[:, r, :] for r in range(PACK)])

        def quantize_w(part, third):
            w_mx[part, third] = quantize("w%s%d" % (part, third), w_grouped[part, third], E4M3)

        def turn_row(j, copies=(scalar, scalar), in_narrow=False):
            sources = [dk[:, j, :]] + [dq[:, j, N * i : N * (i + 1)] for i in range(Q_FEATURES // N)]
            return turn(copies, "row%d_grouped" % j, sources, in_narrow)


        def matmul(bank, stationary, block, moving, start, stop):
            cols = slice(P * block, P * (block + 1))
            nc.tensor.matmul_mx(
                out=bank[:],
                lhsT=stationary[0][:, cols].bitcast(stationary[2]),
                lhsT_scale=stationary[1][:, cols],
                rhs=moving[0][:].bitcast(moving[2]),
                rhs_scale=moving[1][:],
                start=start,
                stop=stop,
            )

        def stage_tile(name, width):
            tile = sb.tile([P, width], F32, name=name, tag="stage", bufs=STAGE_BUFS)
            return tile

        def dw_bank(copy, name, part, third, r, dst):
            bank = psum.tile([P, N], F32, name=name, tag="bank")
            matmul(bank, x_mx[third], r, dz_tokens[part], True, True)
            copy(out=dst, in_=bank[:])

        def dw_half(part, third, half):
            name = "dw%s%d" % (part, third)
            if half == 0:
                stages[name] = stage_tile(name, PACK * N)
            for r in (2 * half, 2 * half + 1):
                dw_bank(scalar, "%s_bank%d" % (name, r), part, third, r, stages[name][:, N * r : N * (r + 1)])
            if half == 1:
                columns = {"k": out_2, "v": out_3, "q0": out_1[:, :N]}[part]
                nc.sync.dma_start(
                    out=columns[N * third : N * (third + 1), :].rearrange("(m r) c -> m r c", r=PACK),
                    in_=four_rows(stages[name]),
                )

        def dw_q12(copy_q2, third, half):
            name = "dwq12_%d_%d" % (third, half)
            stage = stage_tile(name, PACK * N)
            for s in range(2):
                for c, (part, copy) in enumerate((("q1", scalar), ("q2", copy_q2))):
                    i = 2 * s + c
                    dw_bank(copy, "%s_bank%d" % (name, i), part, third, 2 * half + s, stage[:, N * i : N * (i + 1)])
            rows = out_1[N * third : N * (third + 1), N:].rearrange("(m r) c -> m r c", r=PACK)
            nc.sync.dma_start(
                out=rows[:, 2 * half : 2 * half + 2, :], in_=stage[:].rearrange("p (r c) -> p r c", r=2)
            )

        def dx_bank(copy, j, third, stored_together):
            first, last = stored_together[0], stored_together[-1]
            name = "dx%d_%d" % (j, first)
            if third == first:
                stages[name] = stage_tile(name, N * len(stored_together))
            bank = psum.tile([P, N], F32, name="dx%d_bank%d" % (j, third), tag="bank")
            passes = [(dv_features, j, "v")] + [(dz_row[j], i, part) for i, part in enumerate(("k", "q0", "q1", "q2"))]
            for i, (stationary, block, part) in enumerate(passes):
                matmul(bank, stationary, block, w_mx[part, third], i == 0, i == len(passes) - 1)
            place = third - first
            copy(
                out=stages[name][:, N * place : N * (place + 1)].rearrange("p (m r) -> p m r", r=PACK),
                in_=bank[:].rearrange("p (r m) -> p m r", r=PACK),
            )
            if third == last:
                rows = out_0.rearrange("b (p j) e -> p (b j) e", j=PACK)
                nc.sync.dma_start(out=rows[:, j, N * first : N * (last + 1)], in_=stages[name][:])


        tables = sb.tile([P, 3 * TABLE], BF16, name="tables", align_bytes=64)
        nc.sync.dma_start(out=tables[:, :TABLE], in_=freqs_cos.rearrange("(p j) i -> p (j i)", j=PACK))
        nc.sync.dma_start(out=tables[:, TABLE : 2 * TABLE], in_=freqs_sin.rearrange("(p j) i -> p (j i)", j=PACK))
        gk = load_gradient("gk", grad_1)
        dv = load_gradient("dv", grad_2)
        x_rows = load("x", x.rearrange("b (p j) e -> p (b j e)", j=PACK))
        load_wv(0)
        load_wk(0)
        load_wq(0)

        dk_tile = sb.tile([P, PACK * KV_FEATURES], BF16, name="dk", align_bytes=64)
        dq_tile = sb.tile([P, PACK * Q_FEATURES], BF16, name="dq", align_bytes=64)
        dk, dq = four_rows(dk_tile), four_rows(dq_tile)

        nc.vector.tensor_scalar(
            out=tables[:, 2 * TABLE :], in0=tables[:, TABLE : 2 * TABLE], scalar1=-1.0, scalar2=None, op0=ALU.mult
        )
        transposed_bank = psum.tile([P, 3, P], F32, name="transposed_bank", tag="bank")
        transposed = sb.tile([P, 3, P], F32, name="transposed")
        table_bank = psum_keep.tile([P, 3 * P], F32, name="table_bank")
        for kind in (COS, SIN, MINUS_SIN):
            nc.tensor.transpose(
                transposed_bank[:, kind, :], tables[:].bitcast(F32)[:, P * kind : P * (kind + 1)], ident[:]
            )
        nc.scalar.copy(out=transposed[:], in_=transposed_bank[:])
        for kind in (COS, SIN, MINUS_SIN):
            nc.tensor.transpose(table_bank[:, P * kind : P * (kind + 1)], transposed[:, kind, :], ident[:])
        psum_tables = table_bank[:].bitcast(BF16)

        gq = load_gradient("gq", grad_0)
        with_cos = cos_product("k01", tables[:], gk[:, 0:2, :], 0)
        with_sin = sin_product("k01", tables[:], gk[:, 0:2, :], 0)
        rope_sum(nc.gpsimd, with_cos, with_sin, dk[:, 0:2, :])
        with_cos = cos_product("k23", psum_tables, gk[:, 2:4, :], 2)
        with_sin = sin_product("k23", psum_tables, gk[:, 2:4, :], 2)
        load_wv(1)
        dv_by_tokens = group_tokens(scalar, "dv_by_tokens", dv)
        dv_by_features = turn((scalar, scalar), "dv_by_features", [dv[:, j, :] for j in range(PACK)])
        load_wk(1)
        load_wq(1)
        x0_grouped = group_x(vector, 0)
        x1_grouped = group_x(scalar, 1)
        dz_tokens["v"] = quantize("dv_tokens", dv_by_tokens, E5M2)
        x_mx[0] = quantize("x0", x0_grouped, E4M3)
        rope_sum(nc.vector, with_cos, with_sin, dk[:, 2:4, :])
        turn_w("v", 0)
        turn_w("k", 0)
        dw_half("v", 0, 0)
        dw_half("v", 0, 1)
        x_mx[1] = quantize("x1", x1_grouped, E4M3)
        dv_features = quantize("dv_features", dv_by_features, E5M2)
        x2_grouped = group_x(vector, 2)
        quantize_w("v", 0)
        x_mx[2] = quantize("x2", x2_grouped, E4M3)
        dk_by_tokens = group_tokens(vector, "dk_by_tokens", dk)
        quantize_w("k", 0)

        turn_w("q0", 0)
        dw_half("v", 1, 0)
        dz_tokens["k"] = quantize("dk_tokens", dk_by_tokens, E5M2)
        turn_w("q1", 0)
        dw_half("v", 1, 1)
        load_wv(2)
        load_wk(2)
        load_wq(2)
        with_cos = cos_product("row0", psum_tables, gq[:, 0:1, :], 0)
        quantize_w("q0", 0)
        turn_w("q2", 0, (vector, vector))
        dw_half("v", 2, 0)
        quantize_w("q1", 0)
        turn_w("v", 1)
        dw_half("v", 2, 1)
        quantize_w("q2", 0)
        with_sin = sin_product("row0", psum_tables, gq[:, 0:1, :], 0)
        rope_sum(nc.gpsimd, with_cos, with_sin, dq[:, 0:1, :])
        with_cos = cos_product("q0_rest", psum_tables, gq[:, 1:4, :N], 1)
        with_sin = sin_product("q0_rest", psum_tables, gq[:, 1:4, :N], 1)
        rope_sum(nc.gpsimd, with_cos, with_sin, dq[:, 1:4, :N])
        turn_w("k", 1)
        dw_half("k", 0, 0)
        dw_half("k", 0, 1)
        turn_w("q0", 1)
        dw_half("k", 1, 0)
        turn_w("q1", 1, (vector, vector))
        with_cos = cos_product("row1", psum_tables, gq[:, 1:2, N:], 1)
        dw_half("k", 1, 1)
        row0_grouped = turn_row(0, (vector, vector), in_narrow=True)
        dw_half("k", 2, 0)
        dz_row[0] = quantize("row0", row0_grouped, E5M2)
        turn_w("q2", 1)
        dw_half("k", 2, 1)

        q0_by_tokens = group_tokens(vector, "q0_by_tokens", dq[:, :, :N], in_narrow=True)
        quantize_w("v", 1)
        dz_tokens["q0"] = quantize("q0_tokens", q0_by_tokens, E5M2)
        for part in ("k", "q0", "q1", "q2"):
            quantize_w(part, 1)
        dx_bank(scalar, 0, 0, (0, 1))
        turn_w("v", 2)
        dw_half("q0", 0, 0)
        dw_half("q0", 0, 1)
        with_sin = sin_product("row1", psum_tables, gq[:, 1:2, N:], 1)
        rope_sum(nc.gpsimd, with_cos, with_sin, dq[:, 1:2, N:])
        with_cos = cos_product("row2", psum_tables, gq[:, 2:3, N:], 2)
        with_sin = sin_product("row2", psum_tables, gq[:, 2:3, N:], 2)
        rope_sum(nc.gpsimd, with_cos, with_sin, dq[:, 2:3, N:])
        turn_w("k", 2, (scalar, vector))
        with_cos = cos_product("row3", psum_tables, gq[:, 3:4, N:], 3)
        with_sin = sin_product("row3", psum_tables, gq[:, 3:4, N:], 3)
        dx_bank(scalar, 0, 1, (0, 1))
        dw_half("q0", 1, 0)
        turn_w("q0", 2)
        dw_half("q0", 1, 1)
        row1_grouped = turn_row(1, in_narrow=True)
        rope_sum(nc.vector, with_cos, with_sin, dq[:, 3:4, N:])
        dz_row[1] = quantize("row1", row1_grouped, E5M2)
        dw_half("q0", 2, 0)
        dw_half("q0", 2, 1)
        row2_grouped = turn_row(2)

        q1_by_tokens = group_tokens(vector, "q1_by_tokens", dq[:, :, N : 2 * N], in_narrow=True)
        q2_by_tokens = group_tokens(vector, "q2_by_tokens", dq[:, :, 2 * N :], in_narrow=True)
        dz_tokens["q1"] = quantize("q1_tokens", q1_by_tokens, E5M2)
        dz_tokens["q2"] = quantize("q2_tokens", q2_by_tokens, E5M2)
        dz_row[2] = quantize("row2", row2_grouped, E5M2)
        for part in ("v", "k", "q0"):
            quantize_w(part, 2)
        dx_bank(scalar, 1, 0, (0, 1))
        dx_bank(scalar, 1, 1, (0, 1))
        turn_w("q1", 2)
        dw_q12(scalar, 0, 0)
        quantize_w("q1", 2)
        dx_bank(vector, 2, 0, (0,))
        dw_q12(vector, 0, 1)
        turn_w("q2", 2, (vector, vector))
        dw_q12(scalar, 1, 0)
        row3_grouped = turn_row(3, (vector, vector))
        quantize_w("q2", 2)
        dw_q12(scalar, 1, 1)
        dz_row[3] = quantize("row3", row3_grouped, E5M2)

        dx_bank(vector, 0, 2, (2,))
        dw_q12(vector, 2, 0)
        dx_bank(vector, 1, 2, (2,))
        dw_q12(vector, 2, 1)
        dx_bank(vector, 2, 1, (1, 2))
        dx_bank(scalar, 2, 2, (1, 2))
        dx_bank(vector, 3, 0, (0, 1))
        dx_bank(scalar, 3, 1, (0, 1))
        dx_bank(vector, 3, 2, (2,))
